import numpy as np
import ml_dtypes


def mxq(x, axis, fmt="e4m3"):
    dtype, down = {"e4m3": (ml_dtypes.float8_e4m3fn, 7), "e5m2": (ml_dtypes.float8_e5m2, 14)}[fmt]
    v = np.moveaxis(np.asarray(x, np.float32).astype(ml_dtypes.bfloat16).astype(np.float64), axis, -1)
    blocks = v.reshape(v.shape[:-1] + (-1, 32))
    amax = np.abs(blocks).max(-1, keepdims=True)
    byte = np.maximum(np.where(amax > 0, np.frexp(amax)[1] - 1 + 127, 0) - down, 1)
    scale = np.exp2(byte - 127.0)
    codes = (blocks / scale).astype(np.float32).astype(dtype).astype(np.float64)
    return np.moveaxis((codes * scale).reshape(v.shape), -1, axis)


WIDE = False


def mx_kscale(k):
    if not WIDE:
        return np.ones(k)
    levels = np.array([10, -10, 5, -5, 0])
    if k % 512:
        return np.exp2(np.random.permutation(np.resize(levels, k // 32))).repeat(32)
    a = np.empty((k // 512, 16))
    for p in range(k // 512):
        a[p, :8] = np.random.permutation(np.resize(levels, 8))
        for g in range(8):
            far = levels[np.abs(levels - a[p, g]) >= 10]
            a[p, g + 8] = far[np.random.randint(len(far))]
    return np.exp2(a.ravel()).repeat(32)


BF16 = ml_dtypes.bfloat16


def bf(x):
    return np.asarray(x, np.float32).astype(BF16)


def f64(x):
    return np.asarray(x).astype(np.float64)


N, K, H = 1024, 2, 512


def sigmoid(v):
    return 1.0 / (1.0 + np.exp(-v))


def setup_inputs():
    s = mx_kscale(N)
    t = mx_kscale(4 * H)[:H]
    t2 = np.concatenate([t, t])
    t3 = np.concatenate([t, t, t])
    w = 1.0 / np.sqrt(H * (K + 2))
    mh = f64(bf(np.random.standard_normal((N, K, H))))
    tie = mh[:, 0, :] == mh[:, 1, :]
    mh[:, 1, :] = np.where(tie, mh[:, 1, :] - 0.5, mh[:, 1, :])
    mh0 = bf(mh)
    mailbox_c = bf(np.random.standard_normal((N, K, H)) / np.sqrt(K))
    wiou0 = bf(np.random.standard_normal((3 * H, 2 * H)) * w)
    b_iou = bf(np.random.standard_normal((1, 3 * H)) * 0.1)
    wf0 = bf(np.random.standard_normal((H, 2 * H)) * w)
    U_f_b = bf(np.random.standard_normal(H) * 0.1)
    g = bf(np.random.standard_normal((N, 2 * H)) * np.exp2(np.random.randint(-6, 1, (N, 1))) * 8.0 / s[:, None] * t2)
    a = f64(mh0)
    hc = np.concatenate([a.sum(axis=1), a.max(axis=1)], axis=1)
    f = sigmoid(hc @ f64(wf0).T + f64(U_f_b))
    iou = hc @ f64(wiou0).T + f64(b_iou)
    zi, zo, zu = np.split(iou, 3, axis=1)
    c = sigmoid(zi) * np.tanh(zu) + f * f64(mailbox_c).sum(axis=1)
    return {"mailbox_h": bf(f64(mh0) * s[:, None, None]),
            "mailbox_c": mailbox_c,
            "U_iou_w": bf(f64(wiou0) / t3[:, None]),
            "b_iou": b_iou,
            "U_f_w": bf(f64(wf0) / t[:, None]),
            "U_f_b": U_f_b,
            "iou": np.asarray(iou, np.float32),
            "f": np.asarray(f, np.float32),
            "c": np.asarray(c, np.float32),
            "grad_out": g}


def reference(mailbox_h, mailbox_c, U_iou_w, b_iou, U_f_w, U_f_b, iou, f, c, grad_out):
    mh = f64(mailbox_h)
    hc = np.concatenate([mh.sum(axis=1), mh.max(axis=1)], axis=1)
    mcs = f64(mailbox_c).sum(axis=1)
    g = f64(grad_out)
    gh, gc = g[:, :H], g[:, H:]
    zi, zo, zu = np.split(f64(iou), 3, axis=1)
    si, so, tu = sigmoid(zi), sigmoid(zo), np.tanh(zu)
    tc = np.tanh(f64(c))
    ff = f64(f)
    dc = gc + gh * so * (1.0 - tc * tc)
    di = dc * tu * si * (1.0 - si)
    do = gh * tc * so * (1.0 - so)
    du = dc * si * (1.0 - tu * tu)
    df = dc * mcs * ff * (1.0 - ff)
    dz = np.concatenate([di, do, du, df], axis=1)
    wall = np.concatenate([f64(U_iou_w), f64(U_f_w)], axis=0)
    dhc = mxq(dz, 1, "e5m2") @ mxq(wall, 0, "e4m3")
    dw = mxq(dz[:, :3 * H], 0, "e5m2").T @ mxq(hc, 0, "e4m3")
    hit = np.where(mh == mh.max(axis=1, keepdims=True), 1.0, 0.0)
    share = hit / hit.sum(axis=1, keepdims=True)
    dx = dhc[:, None, :H] + dhc[:, None, H:] * share
    return dx, dw

@@ -1,0 +1,343 @@
+from contextlib import ExitStack
+import math
+
+import concourse.mybir as mybir
+from concourse.masks import make_identity
+
+NODES, KIDS, H = 1024, 2, 512
+FLOPS = 2 * NODES * (4 * H) * (2 * H) + 2 * (3 * H) * NODES * (2 * H)
+
+F32 = mybir.dt.float32
+BF16 = mybir.dt.bfloat16
+U32 = mybir.dt.uint32
+U8 = mybir.dt.uint8
+E4 = mybir.dt.float8_e4m3fn_x4
+E5 = mybir.dt.float8_e5m2_x4
+ALU = mybir.AluOpType
+ACT = mybir.ActivationFunctionType
+
+P = 128
+TINY = 2.0 ** -126
+
+CFG = {
+    "ab": (True, True, True, False),
+    "hc_il": "scalar",
+    "w_il": ("scalar", "scalar", "scalar", "scalar"),
+    "nm_il": ("scalar", "scalar", "scalar", "scalar", "scalar", "scalar"),
+    "dw_ev": ("scalar", "vector"),
+    "pe_mcs": True,
+    "o1_bufs": 6,
+    "tc_bufs": 5,
+    "m0_bufs": 3,
+    "order": 0,
+}
+
+
+def tile_treelstmcellv2_t_v_kernel(
+    tc, mailbox_h, mailbox_c, U_iou_w, b_iou, U_f_w, U_f_b, iou, f, c, grad_out, out_0, out_1
+):
+    nc = tc.nc
+    V = nc.vector
+
+    mh_v = mailbox_h.rearrange("(g p j) k h -> p g j (k h)", g=2, j=4)
+    mc_v = mailbox_c.rearrange("(g p j) k h -> p g j (k h)", g=2, j=4)
+    iou_v = iou.rearrange("(g p j) w -> p g j w", g=2, j=4)
+    f_v = f.rearrange("(g p j) w -> p g j w", g=2, j=4)
+    c_v = c.rearrange("(g p j) w -> p g j w", g=2, j=4)
+    go_v = grad_out.rearrange("(g p j) w -> p g j w", g=2, j=4)
+    o0_v = out_0.rearrange("(g p j) k h -> p g j (k h)", g=2, j=4)
+    wiou_v = U_iou_w.rearrange("(a p j) n -> p a j n", a=3, j=4)
+    wf_v = U_f_w.rearrange("(p j) n -> p j n", j=4)
+
+    with ExitStack() as ctx:
+        const = ctx.enter_context(tc.tile_pool(name="const", bufs=1))
+        inp = ctx.enter_context(tc.tile_pool(name="inp", bufs=2))
+        tmp = ctx.enter_context(tc.tile_pool(name="tmp", bufs=2))
+        keep = ctx.enter_context(tc.tile_pool(name="keep", bufs=1))
+        psum = ctx.enter_context(tc.psum_pool(name="psum", bufs=1))
+
+        ident = const.tile([P, P], F32, name="ident", tag="ident")
+        make_identity(nc, ident[:])
+        identb = const.tile([P, P], BF16, name="identb", tag="identb")
+        if CFG["pe_mcs"]:
+            make_identity(nc, identb[:])
+        mhalf = const.tile([P, 1], F32, name="mhalf", tag="mhalf")
+        nc.vector.memset(mhalf[:], -0.5)
+
+        w_c = keep.tile([P, 4, 1024], U32, name="w_c", tag="w_c", align_bytes=64)
+        w_s = keep.tile([P, 4, 1024], U8, name="w_s", tag="w_s", align_bytes=64)
+        hc_c = keep.tile([P, 2, 1024], U32, name="hc_c", tag="hc_c", align_bytes=64)
+        hc_s = keep.tile([P, 2, 1024], U8, name="hc_s", tag="hc_s", align_bytes=64)
+        dzq_c = keep.tile([P, 2, 1536], U32, name="dzq_c", tag="dzq_c", align_bytes=64)
+        dzq_s = keep.tile([P, 2, 1536], U8, name="dzq_s", tag="dzq_s", align_bytes=64)
+
+        st = {}
+        dzn = {}
+        hcn = {}
+        dzt = {}
+        wraw = {}
+
+        def il_copy(eng, out, in_):
+            if eng == "scalar":
+                nc.scalar.copy(out=out, in_=in_)
+            else:
+                nc.vector.tensor_copy(out=out, in_=in_)
+
+        def loads(s):
+            g, jh = divmod(s, 2)
+            js = slice(2 * jh, 2 * jh + 2)
+            iou_t = inp.tile([P, 2, 1536], F32, name="iou_t", tag="iou_t")
+            mh_t = inp.tile([P, 2, 1024], BF16, name="mh_t", tag="mh_t")
+            go_t = inp.tile([P, 2, 1024], BF16, name="go_t", tag="go_t")
+            c_t = inp.tile([P, 2, 512], F32, name="c_t", tag="c_t")
+            mc_t = inp.tile([P, 2, 1024], BF16, name="mc_t", tag="mc_t")
+            f_t = inp.tile([P, 2, 512], F32, name="f_t", tag="f_t")
+            nc.sync.dma_start(out=iou_t[:, :, 512:1024], in_=iou_v[:, g, js, 512:1024])
+            nc.sync.dma_start(out=mh_t[:], in_=mh_v[:, g, js, :])
+            nc.sync.dma_start(out=c_t[:], in_=c_v[:, g, js, :])
+            nc.sync.dma_start(out=go_t[:], in_=go_v[:, g, js, :])
+            nc.sync.dma_start(out=mc_t[:], in_=mc_v[:, g, js, :])
+            nc.sync.dma_start(out=f_t[:], in_=f_v[:, g, js, :])
+            nc.sync.dma_start(out=iou_t[:, :, 0:512], in_=iou_v[:, g, js, 0:512])
+            nc.sync.dma_start(out=iou_t[:, :, 1024:1536], in_=iou_v[:, g, js, 1024:1536])
+            st[s] = {"iou": iou_t, "mh": mh_t, "go": go_t, "c": c_t, "mc": mc_t, "f": f_t}
+
+        def acts(s):
+            d = st[s]
+            zi = d["iou"][:, :, 0:512]
+            zo = d["iou"][:, :, 512:1024]
+            zu = d["iou"][:, :, 1024:1536]
+            hqc = tmp.tile([P, 2, 512], F32, name="hqc", tag="hqc")
+            hqu = tmp.tile([P, 2, 512], F32, name="hqu", tag="hqu")
+            r2 = math.sqrt(0.5)
+            nc.scalar.activation(out=zo, in_=zo, func=ACT.Tanh, scale=0.5)
+            nc.scalar.activation(out=d["c"][:], in_=d["c"][:], func=ACT.Tanh)
+            nc.scalar.activation(out=hqc[:], in_=d["c"][:], func=ACT.Square, scale=r2)
+            nc.scalar.activation(out=d["f"][:], in_=d["f"][:], func=ACT.Square, bias=mhalf[:, 0:1])
+            nc.scalar.activation(out=zi, in_=zi, func=ACT.Tanh, scale=0.5)
+            nc.scalar.activation(out=zu, in_=zu, func=ACT.Tanh)
+            nc.scalar.activation(out=hqu[:], in_=zu, func=ACT.Square, scale=r2)
+            d["hqc"] = hqc
+            d["hqu"] = hqu
+
+        def hm(s):
+            g, jh = divmod(s, 2)
+            js = slice(2 * jh, 2 * jh + 2)
+            d = st[s]
+            if jh == 0:
+                hcn_t = tmp.tile([P, 4, 1024], BF16, name="hcn_t", tag="hcn_t", bufs=1)
+                hcn[g] = hcn_t
+            hn = hcn[g]
+            mh0 = d["mh"][:, :, 0:512]
+            mh1 = d["mh"][:, :, 512:1024]
+            dd = tmp.tile([P, 2, 512], BF16, name="dd", tag="dd", bufs=1)
+            dd2 = tmp.tile([P, 2, 512], BF16, name="dd2", tag="dd2", bufs=1)
+            m0 = tmp.tile([P, 2, 512], BF16, name="m0", tag="m0", bufs=CFG["m0_bufs"])
+            V.tensor_tensor(out=dd[:], in0=mh0, in1=mh1, op=ALU.subtract)
+            V.tensor_tensor(out=hn[:, js, 0:512], in0=mh0, in1=mh1, op=ALU.add)
+            V.tensor_scalar(out=dd2[:], in0=dd[:], scalar1=-TINY, scalar2=TINY, op0=ALU.max, op1=ALU.min)
+            V.tensor_tensor(out=hn[:, js, 512:1024], in0=mh0, in1=mh1, op=ALU.max)
+            V.tensor_scalar(out=m0[:], in0=dd2[:], scalar1=0.5 / TINY, scalar2=0.5, op0=ALU.mult, op1=ALU.add)
+            d["m0"] = m0
+
+        def chain(s):
+            g, jh = divmod(s, 2)
+            js = slice(2 * jh, 2 * jh + 2)
+            d = st[s]
+            if jh == 0:
+                dzn_t = tmp.tile([P, 4, 2048], BF16, name="dzn_t", tag="dzn_t", align_bytes=64)
+                dzn[g] = dzn_t
+            dz = dzn[g]
+            ai = d["iou"][:, :, 0:512]
+            ao = d["iou"][:, :, 512:1024]
+            tu = d["iou"][:, :, 1024:1536]
+            tch = d["c"][:]
+            qf = d["f"]
+            hqc = d["hqc"][:]
+            hqu = d["hqu"][:]
+            gh = d["go"][:, :, 0:512]
+            gc = d["go"][:, :, 512:1024]
+            SUB, MUL, ADD = ALU.subtract, ALU.mult, ALU.add
+
+            def zop():
+                if CFG["pe_mcs"]:
+                    for jl in range(2):
+                        acc = psum.tile([P, 512], F32, name="acc_w", tag="acc_w", bufs=3)
+                        nc.tensor.matmul(out=acc[:], lhsT=identb[:], rhs=d["mc"][:, jl, 0:512], start=True, stop=False)
+                        nc.tensor.matmul(out=acc[:], lhsT=identb[:], rhs=d["mc"][:, jl, 512:1024], start=False, stop=True)
+                        V.scalar_tensor_tensor(out=qf[:, jl, :], in0=qf[:, jl, :], scalar=0.25, in1=acc[:], op0=SUB, op1=MUL)
+                else:
+                    mcs = tmp.tile([P, 2, 512], F32, name="mcs", tag="mcs", bufs=1)
+                    V.tensor_tensor(out=mcs[:], in0=d["mc"][:, :, 0:512], in1=d["mc"][:, :, 512:1024], op=ADD)
+                    V.scalar_tensor_tensor(out=qf[:], in0=qf[:], scalar=0.25, in1=mcs[:], op0=SUB, op1=MUL)
+
+            V.scalar_tensor_tensor(out=tch, in0=ao, scalar=1.0, in1=tch, op0=SUB, op1=MUL)
+            V.scalar_tensor_tensor(out=ao, in0=ao, scalar=1.0, in1=gh, op0=ADD, op1=MUL)
+            zop()
+            V.scalar_tensor_tensor(out=hqc, in0=hqc, scalar=0.5, in1=ao, op0=SUB, op1=MUL)
+            V.scalar_tensor_tensor(out=dz[:, js, 512:1024], in0=tch, scalar=-0.25, in1=ao, op0=MUL, op1=MUL)
+            V.tensor_tensor(out=hqc, in0=hqc, in1=gc, op=SUB)
+            V.scalar_tensor_tensor(out=tu, in0=ai, scalar=1.0, in1=tu, op0=SUB, op1=MUL)
+            V.scalar_tensor_tensor(out=ai, in0=ai, scalar=1.0, in1=hqc, op0=ADD, op1=MUL)
+            if s < 3:
+                V.tensor_tensor(out=dz[:, js, 1536:2048], in0=qf[:], in1=hqc, op=MUL)
+            V.scalar_tensor_tensor(out=dz[:, js, 1024:1536], in0=hqu, scalar=0.5, in1=ai, op0=SUB, op1=MUL)
+            V.scalar_tensor_tensor(out=dz[:, js, 0:512], in0=tu, scalar=0.25, in1=ai, op0=MUL, op1=MUL)
+            if s == 3:
+                V.tensor_tensor(out=dz[:, js, 1536:2048], in0=qf[:], in1=hqc, op=MUL)
+
+        def tr(s):
+            g, jh = divmod(s, 2)
+            for jl in range(2):
+                j = 2 * jh + jl
+                words = dzn[g][:, j, :].bitcast(F32)
+                grouped = tmp.tile([P, 4, 128, 4], BF16, name="grouped", tag="grouped", align_bytes=64)
+                for hh in range(2):
+                    xt = psum.tile([P, 2, 2, 128], F32, name="xt", tag="xt", bufs=2)
+                    for a2 in range(2):
+                        a = 2 * hh + a2
+                        for u in range(2):
+                            nc.tensor.transpose(xt[:, a2, u, :], words[:, 256 * a + u : 256 * (a + 1) : 2], ident[:])
+                    nc.scalar.copy(
+                        out=grouped[:, 2 * hh : 2 * hh + 2, :, :].bitcast(F32),
+                        in_=xt[:].rearrange("p a u r -> p a r u"),
+                    )
+                t_c = tmp.tile([P, 512], U32, name="t_c", tag="t_c", bufs=CFG["tc_bufs"], align_bytes=64)
+                t_s = tmp.tile([P, 512], U8, name="t_s", tag="t_s", bufs=CFG["tc_bufs"], align_bytes=64)
+                V.quantize_mx(out=t_c[:].bitcast(E5), scales=t_s[:], in_=grouped[:].rearrange("p a r t -> p (a r t)"))
+                dzt[(g, j)] = (t_c, t_s)
+
+        def mm(s):
+            g, jh = divmod(s, 2)
+            ab = CFG["ab"][s]
+            for jl in range(2):
+                j = 2 * jh + jl
+                t_c, t_s = dzt[(g, j)]
+                acc_a = psum.tile([P, 512], F32, name="acc_a", tag="acc_a")
+                acc_b = psum.tile([P, 512], F32, name="acc_b", tag="acc_b")
+                acc_ab = psum.tile([P, 512], F32, name="acc_ab", tag="acc_ab") if ab else None
+                for a in range(4):
+                    cols = slice(128 * a, 128 * a + 128)
+                    for nh in range(2):
+                        ncols = slice(512 * nh, 512 * nh + 512)
+                        own = acc_a if nh == 0 else acc_b
+                        nc.tensor.matmul_mx(
+                            out=own[:], lhsT=t_c[:, cols].bitcast(E5), lhsT_scale=t_s[:, cols],
+                            rhs=w_c[:, a, ncols].bitcast(E4), rhs_scale=w_s[:, a, ncols],
+                            start=(a == 0), stop=(a == 3),
+                        )
+                        if ab:
+                            nc.tensor.matmul_mx(
+                                out=acc_ab[:], lhsT=t_c[:, cols].bitcast(E5), lhsT_scale=t_s[:, cols],
+                                rhs=w_c[:, a, ncols].bitcast(E4), rhs_scale=w_s[:, a, ncols],
+                                start=(a == 0 and nh == 0), stop=(a == 3 and nh == 1),
+                            )
+                t0 = tmp.tile([P, 512], F32, name="t0", tag="t0")
+                o0 = tmp.tile([P, 2, 512], F32, name="o0", tag="o0")
+                V.tensor_tensor(out=t0[:], in0=acc_b[:], in1=st[s]["m0"][:, jl, :], op=ALU.mult)
+                if ab:
+                    V.tensor_tensor(out=o0[:, 1, :], in0=acc_ab[:], in1=t0[:], op=ALU.subtract)
+                else:
+                    t1 = tmp.tile([P, 512], F32, name="t1", tag="t1")
+                    V.tensor_tensor(out=t1[:], in0=acc_b[:], in1=t0[:], op=ALU.subtract)
+                V.tensor_tensor(out=o0[:, 0, :], in0=acc_a[:], in1=t0[:], op=ALU.add)
+                if not ab:
+                    V.tensor_tensor(out=o0[:, 1, :], in0=acc_a[:], in1=t1[:], op=ALU.add)
+                nc.sync.dma_start(out=o0_v[:, g, j, :], in_=o0[:].rearrange("p k h -> p (k h)"))
+
+        def wload(pool, a):
+            raw = pool.tile([P, 4, 1024], BF16, name="wraw", tag="wraw")
+            src = wiou_v[:, a, :, :] if a < 3 else wf_v
+            nc.sync.dma_start(out=raw[:], in_=src)
+            wraw[a] = raw
+
+        def wprep(pool, a):
+            for nh in range(2):
+                ncols = slice(512 * nh, 512 * nh + 512)
+                wi = pool.tile([P, 512, 4], BF16, name="wi", tag="wi", align_bytes=64)
+                il_copy(CFG["w_il"][a], wi[:], wraw[a][:, :, ncols].rearrange("p j c -> p c j"))
+                V.quantize_mx(
+                    out=w_c[:, a, ncols].bitcast(E4), scales=w_s[:, a, ncols], in_=wi[:].rearrange("p c j -> p (c j)")
+                )
+
+        def nm(pool, g, a):
+            cols = slice(512 * a, 512 * a + 512)
+            il = pool.tile([P, 512, 4], BF16, name="il", tag="il", bufs=3, align_bytes=64)
+            il_copy(CFG["nm_il"][3 * g + a], il[:], dzn[g][:, :, cols].rearrange("p j c -> p c j"))
+            V.quantize_mx(
+                out=dzq_c[:, g, cols].bitcast(E5), scales=dzq_s[:, g, cols], in_=il[:].rearrange("p c j -> p (c j)")
+            )
+
+        def hcq(pool, g):
+            for nh in range(2):
+                cols = slice(512 * nh, 512 * nh + 512)
+                il = pool.tile([P, 512, 4], BF16, name="il", tag="il", bufs=3, align_bytes=64)
+                il_copy(CFG["hc_il"], il[:], hcn[g][:, :, cols].rearrange("p j c -> p c j"))
+                V.quantize_mx(
+                    out=hc_c[:, g, cols].bitcast(E4), scales=hc_s[:, g, cols], in_=il[:].rearrange("p c j -> p (c j)")
+                )
+
+        def dw(pool, m):
+            cols = slice(128 * m, 128 * m + 128)
+            for nh in range(2):
+                ncols = slice(512 * nh, 512 * nh + 512)
+                acc = psum.tile([P, 512], F32, name="acc_w", tag="acc_w", bufs=3)
+                for g in range(2):
+                    nc.tensor.matmul_mx(
+                        out=acc[:], lhsT=dzq_c[:, g, cols].bitcast(E5), lhsT_scale=dzq_s[:, g, cols],
+                        rhs=hc_c[:, g, ncols].bitcast(E4), rhs_scale=hc_s[:, g, ncols],
+                        start=(g == 0), stop=(g == 1),
+                    )
+                o1 = pool.tile([P, 512], F32, name="o1", tag="o1", bufs=CFG["o1_bufs"])
+                il_copy(CFG["dw_ev"][(m + nh) % len(CFG["dw_ev"])], o1[:], acc[:])
+                nc.sync.dma_start(out=out_1[128 * m : 128 * m + 128, ncols], in_=o1[:])
+
+        with tc.tile_pool(name="wpool", bufs=2) as wpool:
+            loads(0)
+            wload(wpool, 0)
+            wload(wpool, 1)
+            loads(1)
+            acts(0)
+            hm(0)
+            chain(0)
+            wprep(wpool, 0)
+            wload(wpool, 2)
+            wprep(wpool, 1)
+            wload(wpool, 3)
+            acts(1)
+            tr(0)
+            loads(2)
+            hm(1)
+            chain(1)
+            wprep(wpool, 2)
+            wprep(wpool, 3)
+
+        with tc.tile_pool(name="late", bufs=2) as late:
+            acts(2)
+            tr(1)
+            mm(0)
+            mm(1)
+            loads(3)
+            hm(2)
+            chain(2)
+            nm(late, 0, 1)
+            nm(late, 0, 2)
+            nm(late, 0, 0)
+            hcq(late, 0)
+            acts(3)
+            tr(2)
+            mm(2)
+            hm(3)
+            hcq(late, 1)
+            chain(3)
+            nm(late, 1, 1)
+            for m in range(4, 8):
+                dw(late, m)
+            nm(late, 1, 2)
+            for m in range(8, 12):
+                dw(late, m)
+            nm(late, 1, 0)
+            tr(3)
+            mm(3)
+            for m in range(0, 4):
+                dw(late, m)

@@ -21,15 +21,17 @@ TINY = 2.0 ** -126
 
 CFG = {
     "ab": (True, True, True, False),
-    "hc_il": "scalar",
-    "w_il": ("scalar", "scalar", "scalar", "scalar"),
-    "nm_il": ("scalar", "scalar", "scalar", "scalar", "scalar", "scalar"),
-    "dw_ev": ("scalar", "vector"),
-    "pe_mcs": True,
+    "hc_il": ("scalar",) * 4,
+    "w_il": ("pe", "pe", "pe", "scalar"),
+    "nm_il": ("scalar", "scalar", "scalar", "pe", "scalar", "vector"),
+    "dw_ev": ("scalar", "vector") * 4 + ("scalar",) * 8 + ("scalar", "vector") * 4,
+    "pe_mcs": (True,) * 4,
+    "xt_ev": ("scalar",),
+    "pe_ev": "scalar",
     "o1_bufs": 6,
     "tc_bufs": 5,
     "m0_bufs": 3,
-    "order": 0,
+    "accw_bufs": 3,
 }
 
 
@@ -59,8 +61,7 @@ def tile_treelstmcellv2_t_v_kernel(
         ident = const.tile([P, P], F32, name="ident", tag="ident")
         make_identity(nc, ident[:])
         identb = const.tile([P, P], BF16, name="identb", tag="identb")
-        if CFG["pe_mcs"]:
-            make_identity(nc, identb[:])
+        make_identity(nc, identb[:])
         mhalf = const.tile([P, 1], F32, name="mhalf", tag="mhalf")
         nc.vector.memset(mhalf[:], -0.5)
 
@@ -82,6 +83,20 @@ def tile_treelstmcellv2_t_v_kernel(
                 nc.scalar.copy(out=out, in_=in_)
             else:
                 nc.vector.tensor_copy(out=out, in_=in_)
+
+        def interleave(how, dst, src3):
+            if how == "pe":
+                for qq in range(2):
+                    bank = psum.tile([P, 256, 4], BF16, name="acc_w", tag="acc_w", bufs=CFG["accw_bufs"])
+                    for h2 in range(2):
+                        c0 = 256 * qq + 128 * h2
+                        nc.tensor.matmul(
+                            out=bank[:, 128 * h2 : 128 * h2 + 128, :], lhsT=identb[:],
+                            rhs=src3[:, :, c0 : c0 + 128].rearrange("p j c -> p c j"), start=True, stop=True,
+                        )
+                    il_copy(CFG["pe_ev"], dst[:, 256 * qq : 256 * qq + 256, :], bank[:])
+            else:
+                il_copy(how, dst, src3.rearrange("p j c -> p c j"))
 
         def loads(s):
             g, jh = divmod(s, 2)
@@ -140,11 +155,11 @@ def tile_treelstmcellv2_t_v_kernel(
             V.tensor_scalar(out=m0[:], in0=dd2[:], scalar1=0.5 / TINY, scalar2=0.5, op0=ALU.mult, op1=ALU.add)
             d["m0"] = m0
 
-        def chain(s):
+        def chain(s, ks):
             g, jh = divmod(s, 2)
             js = slice(2 * jh, 2 * jh + 2)
             d = st[s]
-            if jh == 0:
+            if g not in dzn:
                 dzn_t = tmp.tile([P, 4, 2048], BF16, name="dzn_t", tag="dzn_t", align_bytes=64)
                 dzn[g] = dzn_t
             dz = dzn[g]
@@ -158,37 +173,42 @@ def tile_treelstmcellv2_t_v_kernel(
             gh = d["go"][:, :, 0:512]
             gc = d["go"][:, :, 512:1024]
             SUB, MUL, ADD = ALU.subtract, ALU.mult, ALU.add
-
-            def zop():
-                if CFG["pe_mcs"]:
-                    for jl in range(2):
-                        acc = psum.tile([P, 512], F32, name="acc_w", tag="acc_w", bufs=3)
-                        nc.tensor.matmul(out=acc[:], lhsT=identb[:], rhs=d["mc"][:, jl, 0:512], start=True, stop=False)
-                        nc.tensor.matmul(out=acc[:], lhsT=identb[:], rhs=d["mc"][:, jl, 512:1024], start=False, stop=True)
-                        V.scalar_tensor_tensor(out=qf[:, jl, :], in0=qf[:, jl, :], scalar=0.25, in1=acc[:], op0=SUB, op1=MUL)
-                else:
+            stt = V.scalar_tensor_tensor
+            for k in ks:
+                if k == "E":
+                    stt(out=tch, in0=ao, scalar=1.0, in1=tch, op0=SUB, op1=MUL)
+                elif k == "Pq":
+                    stt(out=ao, in0=ao, scalar=1.0, in1=gh, op0=ADD, op1=MUL)
+                elif k == "Gt":
+                    stt(out=tu, in0=ai, scalar=1.0, in1=tu, op0=SUB, op1=MUL)
+                elif k == "R":
+                    stt(out=hqc, in0=hqc, scalar=0.5, in1=ao, op0=SUB, op1=MUL)
+                elif k == "Z" and not CFG["pe_mcs"][s]:
                     mcs = tmp.tile([P, 2, 512], F32, name="mcs", tag="mcs", bufs=1)
                     V.tensor_tensor(out=mcs[:], in0=d["mc"][:, :, 0:512], in1=d["mc"][:, :, 512:1024], op=ADD)
-                    V.scalar_tensor_tensor(out=qf[:], in0=qf[:], scalar=0.25, in1=mcs[:], op0=SUB, op1=MUL)
+                    stt(out=qf[:], in0=qf[:], scalar=0.25, in1=mcs[:], op0=SUB, op1=MUL)
+                elif k == "Z":
+                    for jl in range(2):
+                        acc = psum.tile([P, 512], F32, name="acc_w", tag="acc_w", bufs=CFG["accw_bufs"])
+                        nc.tensor.matmul(out=acc[:], lhsT=identb[:], rhs=d["mc"][:, jl, 0:512], start=True, stop=False)
+                        nc.tensor.matmul(out=acc[:], lhsT=identb[:], rhs=d["mc"][:, jl, 512:1024], start=False, stop=True)
+                        stt(out=qf[:, jl, :], in0=qf[:, jl, :], scalar=0.25, in1=acc[:], op0=SUB, op1=MUL)
+                elif k == "ndc":
+                    V.tensor_tensor(out=hqc, in0=hqc, in1=gc, op=SUB)
+                elif k == "do":
+                    stt(out=dz[:, js, 512:1024], in0=tch, scalar=-0.25, in1=ao, op0=MUL, op1=MUL)
+                elif k == "nE":
+                    stt(out=ai, in0=ai, scalar=1.0, in1=hqc, op0=ADD, op1=MUL)
+                elif k == "du":
+                    stt(out=dz[:, js, 1024:1536], in0=hqu, scalar=0.5, in1=ai, op0=SUB, op1=MUL)
+                elif k == "di":
+                    stt(out=dz[:, js, 0:512], in0=tu, scalar=0.25, in1=ai, op0=MUL, op1=MUL)
+                else:
+                    V.tensor_tensor(out=dz[:, js, 1536:2048], in0=qf[:], in1=hqc, op=MUL)
 
-            V.scalar_tensor_tensor(out=tch, in0=ao, scalar=1.0, in1=tch, op0=SUB, op1=MUL)
-            V.scalar_tensor_tensor(out=ao, in0=ao, scalar=1.0, in1=gh, op0=ADD, op1=MUL)
-            zop()
-            V.scalar_tensor_tensor(out=hqc, in0=hqc, scalar=0.5, in1=ao, op0=SUB, op1=MUL)
-            V.scalar_tensor_tensor(out=dz[:, js, 512:1024], in0=tch, scalar=-0.25, in1=ao, op0=MUL, op1=MUL)
-            V.tensor_tensor(out=hqc, in0=hqc, in1=gc, op=SUB)
-            V.scalar_tensor_tensor(out=tu, in0=ai, scalar=1.0, in1=tu, op0=SUB, op1=MUL)
-            V.scalar_tensor_tensor(out=ai, in0=ai, scalar=1.0, in1=hqc, op0=ADD, op1=MUL)
-            if s < 3:
-                V.tensor_tensor(out=dz[:, js, 1536:2048], in0=qf[:], in1=hqc, op=MUL)
-            V.scalar_tensor_tensor(out=dz[:, js, 1024:1536], in0=hqu, scalar=0.5, in1=ai, op0=SUB, op1=MUL)
-            V.scalar_tensor_tensor(out=dz[:, js, 0:512], in0=tu, scalar=0.25, in1=ai, op0=MUL, op1=MUL)
-            if s == 3:
-                V.tensor_tensor(out=dz[:, js, 1536:2048], in0=qf[:], in1=hqc, op=MUL)
-
-        def tr(s):
+        def tr(s, jls=(0, 1)):
             g, jh = divmod(s, 2)
-            for jl in range(2):
+            for jl in jls:
                 j = 2 * jh + jl
                 words = dzn[g][:, j, :].bitcast(F32)
                 grouped = tmp.tile([P, 4, 128, 4], BF16, name="grouped", tag="grouped", align_bytes=64)
@@ -198,19 +218,20 @@ def tile_treelstmcellv2_t_v_kernel(
                         a = 2 * hh + a2
                         for u in range(2):
                             nc.tensor.transpose(xt[:, a2, u, :], words[:, 256 * a + u : 256 * (a + 1) : 2], ident[:])
-                    nc.scalar.copy(
-                        out=grouped[:, 2 * hh : 2 * hh + 2, :, :].bitcast(F32),
-                        in_=xt[:].rearrange("p a u r -> p a r u"),
+                    il_copy(
+                        CFG["xt_ev"][(4 * s + 2 * jl + hh) % len(CFG["xt_ev"])],
+                        grouped[:, 2 * hh : 2 * hh + 2, :, :].bitcast(F32),
+                        xt[:].rearrange("p a u r -> p a r u"),
                     )
                 t_c = tmp.tile([P, 512], U32, name="t_c", tag="t_c", bufs=CFG["tc_bufs"], align_bytes=64)
                 t_s = tmp.tile([P, 512], U8, name="t_s", tag="t_s", bufs=CFG["tc_bufs"], align_bytes=64)
                 V.quantize_mx(out=t_c[:].bitcast(E5), scales=t_s[:], in_=grouped[:].rearrange("p a r t -> p (a r t)"))
                 dzt[(g, j)] = (t_c, t_s)
 
-        def mm(s):
+        def mm(s, jls=(0, 1)):
             g, jh = divmod(s, 2)
             ab = CFG["ab"][s]
-            for jl in range(2):
+            for jl in jls:
                 j = 2 * jh + jl
                 t_c, t_s = dzt[(g, j)]
                 acc_a = psum.tile([P, 512], F32, name="acc_a", tag="acc_a")
@@ -255,7 +276,7 @@ def tile_treelstmcellv2_t_v_kernel(
             for nh in range(2):
                 ncols = slice(512 * nh, 512 * nh + 512)
                 wi = pool.tile([P, 512, 4], BF16, name="wi", tag="wi", align_bytes=64)
-                il_copy(CFG["w_il"][a], wi[:], wraw[a][:, :, ncols].rearrange("p j c -> p c j"))
+                interleave(CFG["w_il"][a], wi[:], wraw[a][:, :, ncols])
                 V.quantize_mx(
                     out=w_c[:, a, ncols].bitcast(E4), scales=w_s[:, a, ncols], in_=wi[:].rearrange("p c j -> p (c j)")
                 )
@@ -263,7 +284,7 @@ def tile_treelstmcellv2_t_v_kernel(
         def nm(pool, g, a):
             cols = slice(512 * a, 512 * a + 512)
             il = pool.tile([P, 512, 4], BF16, name="il", tag="il", bufs=3, align_bytes=64)
-            il_copy(CFG["nm_il"][3 * g + a], il[:], dzn[g][:, :, cols].rearrange("p j c -> p c j"))
+            interleave(CFG["nm_il"][3 * g + a], il[:], dzn[g][:, :, cols])
             V.quantize_mx(
                 out=dzq_c[:, g, cols].bitcast(E5), scales=dzq_s[:, g, cols], in_=il[:].rearrange("p c j -> p (c j)")
             )
@@ -272,7 +293,7 @@ def tile_treelstmcellv2_t_v_kernel(
             for nh in range(2):
                 cols = slice(512 * nh, 512 * nh + 512)
                 il = pool.tile([P, 512, 4], BF16, name="il", tag="il", bufs=3, align_bytes=64)
-                il_copy(CFG["hc_il"], il[:], hcn[g][:, :, cols].rearrange("p j c -> p c j"))
+                interleave(CFG["hc_il"][2 * g + nh], il[:], hcn[g][:, :, cols])
                 V.quantize_mx(
                     out=hc_c[:, g, cols].bitcast(E4), scales=hc_s[:, g, cols], in_=il[:].rearrange("p c j -> p (c j)")
                 )
@@ -281,7 +302,7 @@ def tile_treelstmcellv2_t_v_kernel(
             cols = slice(128 * m, 128 * m + 128)
             for nh in range(2):
                 ncols = slice(512 * nh, 512 * nh + 512)
-                acc = psum.tile([P, 512], F32, name="acc_w", tag="acc_w", bufs=3)
+                acc = psum.tile([P, 512], F32, name="acc_w", tag="acc_w", bufs=CFG["accw_bufs"])
                 for g in range(2):
                     nc.tensor.matmul_mx(
                         out=acc[:], lhsT=dzq_c[:, g, cols].bitcast(E5), lhsT_scale=dzq_s[:, g, cols],
@@ -289,9 +310,10 @@ def tile_treelstmcellv2_t_v_kernel(
                         start=(g == 0), stop=(g == 1),
                     )
                 o1 = pool.tile([P, 512], F32, name="o1", tag="o1", bufs=CFG["o1_bufs"])
-                il_copy(CFG["dw_ev"][(m + nh) % len(CFG["dw_ev"])], o1[:], acc[:])
+                il_copy(CFG["dw_ev"][(2 * m + nh) % len(CFG["dw_ev"])], o1[:], acc[:])
                 nc.sync.dma_start(out=out_1[128 * m : 128 * m + 128, ncols], in_=o1[:])
 
+        C = ("E", "Pq", "Z", "R", "do", "ndc", "Gt", "nE", "df", "du", "di")
         with tc.tile_pool(name="wpool", bufs=2) as wpool:
             loads(0)
             wload(wpool, 0)
@@ -299,7 +321,7 @@ def tile_treelstmcellv2_t_v_kernel(
             loads(1)
             acts(0)
             hm(0)
-            chain(0)
+            chain(0, C)
             wprep(wpool, 0)
             wload(wpool, 2)
             wprep(wpool, 1)
@@ -308,7 +330,7 @@ def tile_treelstmcellv2_t_v_kernel(
             tr(0)
             loads(2)
             hm(1)
-            chain(1)
+            chain(1, C)
             wprep(wpool, 2)
             wprep(wpool, 3)
 
@@ -319,7 +341,7 @@ def tile_treelstmcellv2_t_v_kernel(
             mm(1)
             loads(3)
             hm(2)
-            chain(2)
+            chain(2, C)
             nm(late, 0, 1)
             nm(late, 0, 2)
             nm(late, 0, 0)
@@ -329,14 +351,17 @@ def tile_treelstmcellv2_t_v_kernel(
             mm(2)
             hm(3)
             hcq(late, 1)
-            chain(3)
+            chain(3, ("E", "Pq", "Z", "do"))
             nm(late, 1, 1)
             for m in range(4, 8):
                 dw(late, m)
+            chain(3, ("R", "Gt", "ndc", "nE", "du"))
             nm(late, 1, 2)
             for m in range(8, 12):
                 dw(late, m)
+            chain(3, ("di",))
             nm(late, 1, 0)
+            chain(3, ("df",))
             tr(3)
             mm(3)
             for m in range(0, 4):

@@ -22,8 +22,8 @@ TINY = 2.0 ** -126
 CFG = {
     "ab": (True, True, True, False),
     "hc_il": ("scalar",) * 4,
-    "w_il": ("pe", "pe", "pe", "scalar"),
-    "nm_il": ("scalar", "scalar", "scalar", "pe", "scalar", "vector"),
+    "w_il": ("scalar",) * 4,
+    "nm_il": ("scalar", "scalar", "scalar", "vector", "scalar", "vector"),
     "dw_ev": ("scalar", "vector") * 4 + ("scalar",) * 8 + ("scalar", "vector") * 4,
     "pe_mcs": (True,) * 4,
     "xt_ev": ("scalar",),

@@ -96,7 +96,7 @@ def tile_treelstmcellv2_t_v_kernel(
                         )
                     il_copy(CFG["pe_ev"], dst[:, 256 * qq : 256 * qq + 256, :], bank[:])
             else:
-                il_copy(how, dst, src3.rearrange("p j c -> p c j"))
+                il_copy(how, dst.rearrange("p (c i) j -> p c j i", i=4), src3.rearrange("p j (c i) -> p c j i", i=4))
 
         def loads(s):
             g, jh = divmod(s, 2)

@@ -237,32 +237,27 @@ def tile_treelstmcellv2_t_v_kernel(
                 acc_a = psum.tile([P, 512], F32, name="acc_a", tag="acc_a")
                 acc_b = psum.tile([P, 512], F32, name="acc_b", tag="acc_b")
                 acc_ab = psum.tile([P, 512], F32, name="acc_ab", tag="acc_ab") if ab else None
-                for a in range(4):
-                    cols = slice(128 * a, 128 * a + 128)
-                    for nh in range(2):
-                        ncols = slice(512 * nh, 512 * nh + 512)
-                        own = acc_a if nh == 0 else acc_b
-                        nc.tensor.matmul_mx(
-                            out=own[:], lhsT=t_c[:, cols].bitcast(E5), lhsT_scale=t_s[:, cols],
-                            rhs=w_c[:, a, ncols].bitcast(E4), rhs_scale=w_s[:, a, ncols],
-                            start=(a == 0), stop=(a == 3),
-                        )
-                        if ab:
+                groups = [(acc_b, (1,)), (acc_a, (0,))] + ([(acc_ab, (0, 1))] if ab else [])
+                for bank, halves in groups:
+                    for a in range(4):
+                        cols = slice(128 * a, 128 * a + 128)
+                        for nh in halves:
+                            ncols = slice(512 * nh, 512 * nh + 512)
                             nc.tensor.matmul_mx(
-                                out=acc_ab[:], lhsT=t_c[:, cols].bitcast(E5), lhsT_scale=t_s[:, cols],
+                                out=bank[:], lhsT=t_c[:, cols].bitcast(E5), lhsT_scale=t_s[:, cols],
                                 rhs=w_c[:, a, ncols].bitcast(E4), rhs_scale=w_s[:, a, ncols],
-                                start=(a == 0 and nh == 0), stop=(a == 3 and nh == 1),
+                                start=(a == 0 and nh == halves[0]), stop=(a == 3 and nh == halves[-1]),
                             )
                 t0 = tmp.tile([P, 512], F32, name="t0", tag="t0")
                 o0 = tmp.tile([P, 2, 512], F32, name="o0", tag="o0")
                 V.tensor_tensor(out=t0[:], in0=acc_b[:], in1=st[s]["m0"][:, jl, :], op=ALU.mult)
-                if ab:
-                    V.tensor_tensor(out=o0[:, 1, :], in0=acc_ab[:], in1=t0[:], op=ALU.subtract)
-                else:
+                if not ab:
                     t1 = tmp.tile([P, 512], F32, name="t1", tag="t1")
                     V.tensor_tensor(out=t1[:], in0=acc_b[:], in1=t0[:], op=ALU.subtract)
                 V.tensor_tensor(out=o0[:, 0, :], in0=acc_a[:], in1=t0[:], op=ALU.add)
-                if not ab:
+                if ab:
+                    V.tensor_tensor(out=o0[:, 1, :], in0=acc_ab[:], in1=t0[:], op=ALU.subtract)
+                else:
                     V.tensor_tensor(out=o0[:, 1, :], in0=acc_a[:], in1=t1[:], op=ALU.add)
                 nc.sync.dma_start(out=o0_v[:, g, j, :], in_=o0[:].rearrange("p k h -> p (k h)"))
 
@@ -330,9 +325,9 @@ def tile_treelstmcellv2_t_v_kernel(
             tr(0)
             loads(2)
             hm(1)
-            chain(1, C)
             wprep(wpool, 2)
             wprep(wpool, 3)
+            chain(1, C)
 
         with tc.tile_pool(name="late", bufs=2) as late:
             acts(2)

from contextlib import ExitStack
import math

import concourse.mybir as mybir
from concourse.masks import make_identity

NODES, KIDS, H = 1024, 2, 512
FLOPS = 2 * NODES * (4 * H) * (2 * H) + 2 * (3 * H) * NODES * (2 * H)

F32 = mybir.dt.float32
BF16 = mybir.dt.bfloat16
U32 = mybir.dt.uint32
U8 = mybir.dt.uint8
E4 = mybir.dt.float8_e4m3fn_x4
E5 = mybir.dt.float8_e5m2_x4
ALU = mybir.AluOpType
ACT = mybir.ActivationFunctionType

P = 128
TINY = 2.0 ** -126

CFG = {
    "ab": (True, True, True, False),
    "hc_il": ("scalar",) * 4,
    "w_il": ("scalar",) * 4,
    "nm_il": ("scalar", "scalar", "scalar", "vector", "scalar", "vector"),
    "dw_ev": ("scalar", "vector") * 4 + ("scalar",) * 8 + ("scalar", "vector") * 4,
    "pe_mcs": (True,) * 4,
    "xt_ev": ("scalar",),
    "pe_ev": "scalar",
    "o1_bufs": 6,
    "tc_bufs": 5,
    "m0_bufs": 3,
    "accw_bufs": 3,
}


def tile_treelstmcellv2_t_v_kernel(
    tc, mailbox_h, mailbox_c, U_iou_w, b_iou, U_f_w, U_f_b, iou, f, c, grad_out, out_0, out_1
):
    nc = tc.nc
    V = nc.vector

    mh_v = mailbox_h.rearrange("(g p j) k h -> p g j (k h)", g=2, j=4)
    mc_v = mailbox_c.rearrange("(g p j) k h -> p g j (k h)", g=2, j=4)
    iou_v = iou.rearrange("(g p j) w -> p g j w", g=2, j=4)
    f_v = f.rearrange("(g p j) w -> p g j w", g=2, j=4)
    c_v = c.rearrange("(g p j) w -> p g j w", g=2, j=4)
    go_v = grad_out.rearrange("(g p j) w -> p g j w", g=2, j=4)
    o0_v = out_0.rearrange("(g p j) k h -> p g j (k h)", g=2, j=4)
    wiou_v = U_iou_w.rearrange("(a p j) n -> p a j n", a=3, j=4)
    wf_v = U_f_w.rearrange("(p j) n -> p j n", j=4)

    with ExitStack() as ctx:
        const = ctx.enter_context(tc.tile_pool(name="const", bufs=1))
        inp = ctx.enter_context(tc.tile_pool(name="inp", bufs=2))
        tmp = ctx.enter_context(tc.tile_pool(name="tmp", bufs=2))
        keep = ctx.enter_context(tc.tile_pool(name="keep", bufs=1))
        psum = ctx.enter_context(tc.psum_pool(name="psum", bufs=1))

        ident = const.tile([P, P], F32, name="ident", tag="ident")
        make_identity(nc, ident[:])
        identb = const.tile([P, P], BF16, name="identb", tag="identb")
        make_identity(nc, identb[:])
        mhalf = const.tile([P, 1], F32, name="mhalf", tag="mhalf")
        nc.vector.memset(mhalf[:], -0.5)

        w_c = keep.tile([P, 4, 1024], U32, name="w_c", tag="w_c", align_bytes=64)
        w_s = keep.tile([P, 4, 1024], U8, name="w_s", tag="w_s", align_bytes=64)
        hc_c = keep.tile([P, 2, 1024], U32, name="hc_c", tag="hc_c", align_bytes=64)
        hc_s = keep.tile([P, 2, 1024], U8, name="hc_s", tag="hc_s", align_bytes=64)
        dzq_c = keep.tile([P, 2, 1536], U32, name="dzq_c", tag="dzq_c", align_bytes=64)
        dzq_s = keep.tile([P, 2, 1536], U8, name="dzq_s", tag="dzq_s", align_bytes=64)

        st = {}
        dzn = {}
        hcn = {}
        dzt = {}
        wraw = {}

        def il_copy(eng, out, in_):
            if eng == "scalar":
                nc.scalar.copy(out=out, in_=in_)
            else:
                nc.vector.tensor_copy(out=out, in_=in_)

        def interleave(how, dst, src3):
            if how == "pe":
                for qq in range(2):
                    bank = psum.tile([P, 256, 4], BF16, name="acc_w", tag="acc_w", bufs=CFG["accw_bufs"])
                    for h2 in range(2):
                        c0 = 256 * qq + 128 * h2
                        nc.tensor.matmul(
                            out=bank[:, 128 * h2 : 128 * h2 + 128, :], lhsT=identb[:],
                            rhs=src3[:, :, c0 : c0 + 128].rearrange("p j c -> p c j"), start=True, stop=True,
                        )
                    il_copy(CFG["pe_ev"], dst[:, 256 * qq : 256 * qq + 256, :], bank[:])
            else:
                il_copy(how, dst.rearrange("p (c i) j -> p c j i", i=4), src3.rearrange("p j (c i) -> p c j i", i=4))

        def loads(s):
            g, jh = divmod(s, 2)
            js = slice(2 * jh, 2 * jh + 2)
            iou_t = inp.tile([P, 2, 1536], F32, name="iou_t", tag="iou_t")
            mh_t = inp.tile([P, 2, 1024], BF16, name="mh_t", tag="mh_t")
            go_t = inp.tile([P, 2, 1024], BF16, name="go_t", tag="go_t")
            c_t = inp.tile([P, 2, 512], F32, name="c_t", tag="c_t")
            mc_t = inp.tile([P, 2, 1024], BF16, name="mc_t", tag="mc_t")
            f_t = inp.tile([P, 2, 512], F32, name="f_t", tag="f_t")
            nc.sync.dma_start(out=iou_t[:, :, 512:1024], in_=iou_v[:, g, js, 512:1024])
            nc.sync.dma_start(out=mh_t[:], in_=mh_v[:, g, js, :])
            nc.sync.dma_start(out=c_t[:], in_=c_v[:, g, js, :])
            nc.sync.dma_start(out=go_t[:], in_=go_v[:, g, js, :])
            nc.sync.dma_start(out=mc_t[:], in_=mc_v[:, g, js, :])
            nc.sync.dma_start(out=f_t[:], in_=f_v[:, g, js, :])
            nc.sync.dma_start(out=iou_t[:, :, 0:512], in_=iou_v[:, g, js, 0:512])
            nc.sync.dma_start(out=iou_t[:, :, 1024:1536], in_=iou_v[:, g, js, 1024:1536])
            st[s] = {"iou": iou_t, "mh": mh_t, "go": go_t, "c": c_t, "mc": mc_t, "f": f_t}

        def acts(s):
            d = st[s]
            zi = d["iou"][:, :, 0:512]
            zo = d["iou"][:, :, 512:1024]
            zu = d["iou"][:, :, 1024:1536]
            hqc = tmp.tile([P, 2, 512], F32, name="hqc", tag="hqc")
            hqu = tmp.tile([P, 2, 512], F32, name="hqu", tag="hqu")
            r2 = math.sqrt(0.5)
            nc.scalar.activation(out=zo, in_=zo, func=ACT.Tanh, scale=0.5)
            nc.scalar.activation(out=d["c"][:], in_=d["c"][:], func=ACT.Tanh)
            nc.scalar.activation(out=hqc[:], in_=d["c"][:], func=ACT.Square, scale=r2)
            nc.scalar.activation(out=d["f"][:], in_=d["f"][:], func=ACT.Square, bias=mhalf[:, 0:1])
            nc.scalar.activation(out=zi, in_=zi, func=ACT.Tanh, scale=0.5)
            nc.scalar.activation(out=zu, in_=zu, func=ACT.Tanh)
            nc.scalar.activation(out=hqu[:], in_=zu, func=ACT.Square, scale=r2)
            d["hqc"] = hqc
            d["hqu"] = hqu

        def hm(s):
            g, jh = divmod(s, 2)
            js = slice(2 * jh, 2 * jh + 2)
            d = st[s]
            if jh == 0:
                hcn_t = tmp.tile([P, 4, 1024], BF16, name="hcn_t", tag="hcn_t", bufs=1)
                hcn[g] = hcn_t
            hn = hcn[g]
            mh0 = d["mh"][:, :, 0:512]
            mh1 = d["mh"][:, :, 512:1024]
            dd = tmp.tile([P, 2, 512], BF16, name="dd", tag="dd", bufs=1)
            dd2 = tmp.tile([P, 2, 512], BF16, name="dd2", tag="dd2", bufs=1)
            m0 = tmp.tile([P, 2, 512], BF16, name="m0", tag="m0", bufs=CFG["m0_bufs"])
            V.tensor_tensor(out=dd[:], in0=mh0, in1=mh1, op=ALU.subtract)
            V.tensor_tensor(out=hn[:, js, 0:512], in0=mh0, in1=mh1, op=ALU.add)
            V.tensor_scalar(out=dd2[:], in0=dd[:], scalar1=-TINY, scalar2=TINY, op0=ALU.max, op1=ALU.min)
            V.tensor_tensor(out=hn[:, js, 512:1024], in0=mh0, in1=mh1, op=ALU.max)
            V.tensor_scalar(out=m0[:], in0=dd2[:], scalar1=0.5 / TINY, scalar2=0.5, op0=ALU.mult, op1=ALU.add)
            d["m0"] = m0

        def chain(s, ks):
            g, jh = divmod(s, 2)
            js = slice(2 * jh, 2 * jh + 2)
            d = st[s]
            if g not in dzn:
                dzn_t = tmp.tile([P, 4, 2048], BF16, name="dzn_t", tag="dzn_t", align_bytes=64)
                dzn[g] = dzn_t
            dz = dzn[g]
            ai = d["iou"][:, :, 0:512]
            ao = d["iou"][:, :, 512:1024]
            tu = d["iou"][:, :, 1024:1536]
            tch = d["c"][:]
            qf = d["f"]
            hqc = d["hqc"][:]
            hqu = d["hqu"][:]
            gh = d["go"][:, :, 0:512]
            gc = d["go"][:, :, 512:1024]
            SUB, MUL, ADD = ALU.subtract, ALU.mult, ALU.add
            stt = V.scalar_tensor_tensor
            for k in ks:
                if k == "E":
                    stt(out=tch, in0=ao, scalar=1.0, in1=tch, op0=SUB, op1=MUL)
                elif k == "Pq":
                    stt(out=ao, in0=ao, scalar=1.0, in1=gh, op0=ADD, op1=MUL)
                elif k == "Gt":
                    stt(out=tu, in0=ai, scalar=1.0, in1=tu, op0=SUB, op1=MUL)
                elif k == "R":
                    stt(out=hqc, in0=hqc, scalar=0.5, in1=ao, op0=SUB, op1=MUL)
                elif k == "Z" and not CFG["pe_mcs"][s]:
                    mcs = tmp.tile([P, 2, 512], F32, name="mcs", tag="mcs", bufs=1)
                    V.tensor_tensor(out=mcs[:], in0=d["mc"][:, :, 0:512], in1=d["mc"][:, :, 512:1024], op=ADD)
                    stt(out=qf[:], in0=qf[:], scalar=0.25, in1=mcs[:], op0=SUB, op1=MUL)
                elif k == "Z":
                    for jl in range(2):
                        acc = psum.tile([P, 512], F32, name="acc_w", tag="acc_w", bufs=CFG["accw_bufs"])
                        nc.tensor.matmul(out=acc[:], lhsT=identb[:], rhs=d["mc"][:, jl, 0:512], start=True, stop=False)
                        nc.tensor.matmul(out=acc[:], lhsT=identb[:], rhs=d["mc"][:, jl, 512:1024], start=False, stop=True)
                        stt(out=qf[:, jl, :], in0=qf[:, jl, :], scalar=0.25, in1=acc[:], op0=SUB, op1=MUL)
                elif k == "ndc":
                    V.tensor_tensor(out=hqc, in0=hqc, in1=gc, op=SUB)
                elif k == "do":
                    stt(out=dz[:, js, 512:1024], in0=tch, scalar=-0.25, in1=ao, op0=MUL, op1=MUL)
                elif k == "nE":
                    stt(out=ai, in0=ai, scalar=1.0, in1=hqc, op0=ADD, op1=MUL)
                elif k == "du":
                    stt(out=dz[:, js, 1024:1536], in0=hqu, scalar=0.5, in1=ai, op0=SUB, op1=MUL)
                elif k == "di":
                    stt(out=dz[:, js, 0:512], in0=tu, scalar=0.25, in1=ai, op0=MUL, op1=MUL)
                else:
                    V.tensor_tensor(out=dz[:, js, 1536:2048], in0=qf[:], in1=hqc, op=MUL)

        def tr(s, jls=(0, 1)):
            g, jh = divmod(s, 2)
            for jl in jls:
                j = 2 * jh + jl
                words = dzn[g][:, j, :].bitcast(F32)
                grouped = tmp.tile([P, 4, 128, 4], BF16, name="grouped", tag="grouped", align_bytes=64)
                for hh in range(2):
                    xt = psum.tile([P, 2, 2, 128], F32, name="xt", tag="xt", bufs=2)
                    for a2 in range(2):
                        a = 2 * hh + a2
                        for u in range(2):
                            nc.tensor.transpose(xt[:, a2, u, :], words[:, 256 * a + u : 256 * (a + 1) : 2], ident[:])
                    il_copy(
                        CFG["xt_ev"][(4 * s + 2 * jl + hh) % len(CFG["xt_ev"])],
                        grouped[:, 2 * hh : 2 * hh + 2, :, :].bitcast(F32),
                        xt[:].rearrange("p a u r -> p a r u"),
                    )
                t_c = tmp.tile([P, 512], U32, name="t_c", tag="t_c", bufs=CFG["tc_bufs"], align_bytes=64)
                t_s = tmp.tile([P, 512], U8, name="t_s", tag="t_s", bufs=CFG["tc_bufs"], align_bytes=64)
                V.quantize_mx(out=t_c[:].bitcast(E5), scales=t_s[:], in_=grouped[:].rearrange("p a r t -> p (a r t)"))
                dzt[(g, j)] = (t_c, t_s)

        def mm(s, jls=(0, 1)):
            g, jh = divmod(s, 2)
            ab = CFG["ab"][s]
            for jl in jls:
                j = 2 * jh + jl
                t_c, t_s = dzt[(g, j)]
                acc_a = psum.tile([P, 512], F32, name="acc_a", tag="acc_a")
                acc_b = psum.tile([P, 512], F32, name="acc_b", tag="acc_b")
                acc_ab = psum.tile([P, 512], F32, name="acc_ab", tag="acc_ab") if ab else None
                groups = [(acc_b, (1,)), (acc_a, (0,))] + ([(acc_ab, (0, 1))] if ab else [])
                for bank, halves in groups:
                    for a in range(4):
                        cols = slice(128 * a, 128 * a + 128)
                        for nh in halves:
                            ncols = slice(512 * nh, 512 * nh + 512)
                            nc.tensor.matmul_mx(
                                out=bank[:], lhsT=t_c[:, cols].bitcast(E5), lhsT_scale=t_s[:, cols],
                                rhs=w_c[:, a, ncols].bitcast(E4), rhs_scale=w_s[:, a, ncols],
                                start=(a == 0 and nh == halves[0]), stop=(a == 3 and nh == halves[-1]),
                            )
                t0 = tmp.tile([P, 512], F32, name="t0", tag="t0")
                o0 = tmp.tile([P, 2, 512], F32, name="o0", tag="o0")
                V.tensor_tensor(out=t0[:], in0=acc_b[:], in1=st[s]["m0"][:, jl, :], op=ALU.mult)
                if not ab:
                    t1 = tmp.tile([P, 512], F32, name="t1", tag="t1")
                    V.tensor_tensor(out=t1[:], in0=acc_b[:], in1=t0[:], op=ALU.subtract)
                V.tensor_tensor(out=o0[:, 0, :], in0=acc_a[:], in1=t0[:], op=ALU.add)
                if ab:
                    V.tensor_tensor(out=o0[:, 1, :], in0=acc_ab[:], in1=t0[:], op=ALU.subtract)
                else:
                    V.tensor_tensor(out=o0[:, 1, :], in0=acc_a[:], in1=t1[:], op=ALU.add)
                nc.sync.dma_start(out=o0_v[:, g, j, :], in_=o0[:].rearrange("p k h -> p (k h)"))

        def wload(pool, a):
            raw = pool.tile([P, 4, 1024], BF16, name="wraw", tag="wraw")
            src = wiou_v[:, a, :, :] if a < 3 else wf_v
            nc.sync.dma_start(out=raw[:], in_=src)
            wraw[a] = raw

        def wprep(pool, a):
            for nh in range(2):
                ncols = slice(512 * nh, 512 * nh + 512)
                wi = pool.tile([P, 512, 4], BF16, name="wi", tag="wi", align_bytes=64)
                interleave(CFG["w_il"][a], wi[:], wraw[a][:, :, ncols])
                V.quantize_mx(
                    out=w_c[:, a, ncols].bitcast(E4), scales=w_s[:, a, ncols], in_=wi[:].rearrange("p c j -> p (c j)")
                )

        def nm(pool, g, a):
            cols = slice(512 * a, 512 * a + 512)
            il = pool.tile([P, 512, 4], BF16, name="il", tag="il", bufs=3, align_bytes=64)
            interleave(CFG["nm_il"][3 * g + a], il[:], dzn[g][:, :, cols])
            V.quantize_mx(
                out=dzq_c[:, g, cols].bitcast(E5), scales=dzq_s[:, g, cols], in_=il[:].rearrange("p c j -> p (c j)")
            )

        def hcq(pool, g):
            for nh in range(2):
                cols = slice(512 * nh, 512 * nh + 512)
                il = pool.tile([P, 512, 4], BF16, name="il", tag="il", bufs=3, align_bytes=64)
                interleave(CFG["hc_il"][2 * g + nh], il[:], hcn[g][:, :, cols])
                V.quantize_mx(
                    out=hc_c[:, g, cols].bitcast(E4), scales=hc_s[:, g, cols], in_=il[:].rearrange("p c j -> p (c j)")
                )

        def dw(pool, m):
            cols = slice(128 * m, 128 * m + 128)
            for nh in range(2):
                ncols = slice(512 * nh, 512 * nh + 512)
                acc = psum.tile([P, 512], F32, name="acc_w", tag="acc_w", bufs=CFG["accw_bufs"])
                for g in range(2):
                    nc.tensor.matmul_mx(
                        out=acc[:], lhsT=dzq_c[:, g, cols].bitcast(E5), lhsT_scale=dzq_s[:, g, cols],
                        rhs=hc_c[:, g, ncols].bitcast(E4), rhs_scale=hc_s[:, g, ncols],
                        start=(g == 0), stop=(g == 1),
                    )
                o1 = pool.tile([P, 512], F32, name="o1", tag="o1", bufs=CFG["o1_bufs"])
                il_copy(CFG["dw_ev"][(2 * m + nh) % len(CFG["dw_ev"])], o1[:], acc[:])
                nc.sync.dma_start(out=out_1[128 * m : 128 * m + 128, ncols], in_=o1[:])

        C = ("E", "Pq", "Z", "R", "do", "ndc", "Gt", "nE", "df", "du", "di")
        with tc.tile_pool(name="wpool", bufs=2) as wpool:
            loads(0)
            wload(wpool, 0)
            wload(wpool, 1)
            loads(1)
            acts(0)
            hm(0)
            chain(0, C)
            wprep(wpool, 0)
            wload(wpool, 2)
            wprep(wpool, 1)
            wload(wpool, 3)
            acts(1)
            tr(0)
            loads(2)
            hm(1)
            wprep(wpool, 2)
            wprep(wpool, 3)
            chain(1, C)

        with tc.tile_pool(name="late", bufs=2) as late:
            acts(2)
            tr(1)
            mm(0)
            mm(1)
            loads(3)
            hm(2)
            chain(2, C)
            nm(late, 0, 1)
            nm(late, 0, 2)
            nm(late, 0, 0)
            hcq(late, 0)
            acts(3)
            tr(2)
            mm(2)
            hm(3)
            hcq(late, 1)
            chain(3, ("E", "Pq", "Z", "do"))
            nm(late, 1, 1)
            for m in range(4, 8):
                dw(late, m)
            chain(3, ("R", "Gt", "ndc", "nE", "du"))
            nm(late, 1, 2)
            for m in range(8, 12):
                dw(late, m)
            chain(3, ("di",))
            nm(late, 1, 0)
            chain(3, ("df",))
            tr(3)
            mm(3)
            for m in range(0, 4):
                dw(late, m)
